import numpy as np
import ml_dtypes


def mxq(x, axis, fmt="e4m3"):
    dtype, down = {"e4m3": (ml_dtypes.float8_e4m3fn, 7), "e5m2": (ml_dtypes.float8_e5m2, 14)}[fmt]
    v = np.moveaxis(np.asarray(x, np.float32).astype(ml_dtypes.bfloat16).astype(np.float64), axis, -1)
    blocks = v.reshape(v.shape[:-1] + (-1, 32))
    amax = np.abs(blocks).max(-1, keepdims=True)
    byte = np.maximum(np.where(amax > 0, np.frexp(amax)[1] - 1 + 127, 0) - down, 1)
    scale = np.exp2(byte - 127.0)
    codes = (blocks / scale).astype(np.float32).astype(dtype).astype(np.float64)
    return np.moveaxis((codes * scale).reshape(v.shape), -1, axis)


WIDE = False


def mx_kscale(k):
    if not WIDE:
        return np.ones(k)
    levels = np.array([10, -10, 5, -5, 0])
    a = np.random.permutation(np.resize(levels, k // 512 * 4)).reshape(k // 512, 4)
    idx = np.arange(k)
    return np.exp2(a[idx // 512, idx % 128 // 32])


BF16 = ml_dtypes.bfloat16


def bf(x):
    return np.asarray(x, np.float32).astype(BF16)


def f64(x):
    return np.asarray(x).astype(np.float64)


E2M1 = np.array([0.0, 0.5, 1.0, 1.5, 2.0, 3.0, 4.0, 6.0, -0.0, -0.5, -1.0, -1.5, -2.0, -3.0, -4.0, -6.0])


def pack_weight(w, fmt):
    k, n = w.shape
    w = f64(bf(w)).reshape(k // 32, 32, n)
    amax = np.abs(w).max(1)
    if fmt == "e4m3":
        byte = np.frexp(amax)[1] - 1 + 127 - 7
    else:
        mant, ex = np.frexp(amax / 6.0)
        byte = np.where(mant > 0.5, ex, ex - 1) + 127
    byte = np.clip(np.where(amax > 0, byte, 1), 1, 254)
    scaled = (w * np.exp2(127.0 - byte)[:, None, :]).reshape(k, n).astype(np.float32)
    by_word = np.ascontiguousarray(scaled.reshape(k // 512, 128, 4, n).transpose(0, 1, 3, 2))
    if fmt == "e4m3":
        words = by_word.astype(ml_dtypes.float8_e4m3fn).view(np.uint8)
    else:
        c = by_word.astype(ml_dtypes.float4_e2m1fn).view(np.uint8) & 0xF
        words = c[..., 0::2] | (c[..., 1::2] << 4)
    return np.ascontiguousarray(words), np.ascontiguousarray(byte.astype(np.uint8).reshape(k // 512, 16, n))


def unpack_weight(words, scales, fmt):
    g, p, n, _ = words.shape
    if fmt == "e4m3":
        vals = np.ascontiguousarray(words).view(ml_dtypes.float8_e4m3fn).astype(np.float64)
    else:
        nib = np.empty((g, p, n, 4), np.uint8)
        nib[..., 0::2] = words & 0xF
        nib[..., 1::2] = words >> 4
        vals = E2M1[nib]
    vals = vals * np.repeat(np.exp2(scales.astype(np.float64) - 127.0), 8, axis=1)[..., None]
    return vals.transpose(0, 1, 3, 2).reshape(g * 512, n)


N, K, H = 128, 2, 1536


def sigmoid(v):
    return 1.0 / (1.0 + np.exp(-v))


def setup_inputs():
    s = mx_kscale(2 * H)[:H]
    s2 = np.concatenate([s, s])
    w = 1.0 / np.sqrt(H * (K + 2))
    mailbox_h = bf(np.random.standard_normal((N, K, H)) * s)
    mailbox_c = bf(np.random.standard_normal((N, K, H)) / np.sqrt(K))
    U_iou_w_words, U_iou_w_scales = pack_weight(np.ascontiguousarray((np.random.standard_normal((3 * H, 2 * H)) * w / s2).T), "e4m3")
    b_iou = bf(np.random.standard_normal((1, 3 * H)) * 0.1)
    U_f_w_words, U_f_w_scales = pack_weight(np.ascontiguousarray((np.random.standard_normal((H, 2 * H)) * w / s2).T), "e4m3")
    U_f_b = bf(np.random.standard_normal(H) * 0.1)
    return {"mailbox_h": mailbox_h,
            "mailbox_c": mailbox_c,
            "U_iou_w_words": U_iou_w_words,
            "U_iou_w_scales": U_iou_w_scales,
            "b_iou": b_iou,
            "U_f_w_words": U_f_w_words,
            "U_f_w_scales": U_f_w_scales,
            "U_f_b": U_f_b}


def reference(mailbox_h, mailbox_c, U_iou_w_words, U_iou_w_scales, b_iou, U_f_w_words, U_f_w_scales, U_f_b):
    mh = f64(mailbox_h)
    mc = f64(mailbox_c)
    h_cat = mh.sum(axis=1)
    h_max = mh.max(axis=1)
    h_combined = np.concatenate([h_cat, h_max], axis=1)
    hq = mxq(h_combined, 1, "e4m3")
    f = sigmoid((hq @ unpack_weight(U_f_w_words, U_f_w_scales, "e4m3")) + f64(U_f_b))
    c_agg = np.sum(f[:, None, :] * mc, axis=1)
    iou = hq @ unpack_weight(U_iou_w_words, U_iou_w_scales, "e4m3")
    iou = iou + f64(b_iou)
    i, o, u = np.split(iou, 3, axis=1)
    c = sigmoid(i) * np.tanh(u) + c_agg
    h = sigmoid(o) * np.tanh(c)
    return np.concatenate([h, c], axis=1)

@@ -1,0 +1,180 @@
+from contextlib import ExitStack
+
+import concourse.mybir as mybir
+from concourse.masks import make_identity
+
+BF16 = mybir.dt.bfloat16
+F32 = mybir.dt.float32
+I32 = mybir.dt.int32
+U32 = mybir.dt.uint32
+U8 = mybir.dt.uint8
+FP8X4 = mybir.dt.float8_e4m3fn_x4
+ALU = mybir.AluOpType
+ACT = mybir.ActivationFunctionType
+
+P = 128
+H = 1536
+G = 6
+FLOPS = 2 * 128 * (2 * H) * (4 * H)
+
+SCALES_ON_GPSIMD = True
+
+
+def tile_treelstmcellv2_w_kernel(
+    tc, mailbox_h, mailbox_c, U_iou_w_words, U_iou_w_scales, b_iou, U_f_w_words, U_f_w_scales, U_f_b, out
+):
+    nc = tc.nc
+    with ExitStack() as ctx:
+        keep = ctx.enter_context(tc.tile_pool(name="keep", bufs=1))
+        work = ctx.enter_context(tc.tile_pool(name="work", bufs=3))
+        psum = ctx.enter_context(tc.psum_pool(name="psum", bufs=8))
+
+        full = [(0, 512), (512, 512), (1024, 512)]
+        tail = [(0, 512), (512, 512), (1024, 256), (1280, 256)]
+        gates = [
+            ("f", U_f_w_words, 0, 9, full),
+            ("i", U_iou_w_words, 0, 0, full),
+            ("u", U_iou_w_words, 2 * H, 6, full),
+            ("o", U_iou_w_words, H, 3, tail),
+        ]
+
+        pf = keep.tile([P, 2, H], U8, name="pf", align_bytes=64)
+        piou = keep.tile([P, 2, 3 * H], U8, name="piou", align_bytes=64)
+        brow = keep.tile([P, 512], BF16, name="brow")
+        nc.vector.memset(brow[:].bitcast(I32), 0)
+        nc.vector.memset(pf[:].bitcast(I32), 0)
+        nc.vector.memset(piou[:].bitcast(I32), 0)
+        ident = keep.tile([P, P], BF16, name="ident")
+        make_identity(nc, ident[:])
+
+        mh = keep.tile([P, 2, H], BF16, name="mh", tag="mh")
+        nc.sync.dma_start(out=mh[:], in_=mailbox_h)
+        nc.scalar.dma_start(out=brow[0:9, :], in_=b_iou.rearrange("o (j n) -> (o j) n", n=512))
+        nc.scalar.dma_start(out=brow[9:12, :], in_=U_f_b.rearrange("(j n) -> j n", n=512))
+
+        def load_planes(plane, scales):
+            for a, g0, g1 in ((0, 0, 4), (1, 4, 6)):
+                rows = 4 * (g1 - g0)
+                for q in range(4):
+                    dst = plane[32 * q : 32 * q + rows, a, :]
+                    src = scales[g0:g1, 4 * q : 4 * q + 4, :]
+                    if SCALES_ON_GPSIMD:
+                        nc.gpsimd.dma_start(out=dst.bitcast(F32), in_=src.bitcast(F32))
+                    else:
+                        nc.sync.dma_start(out=dst.bitcast(I32), in_=src.bitcast(I32))
+
+        load_planes(pf, U_f_w_scales)
+        load_planes(piou, U_iou_w_scales)
+
+        mc = keep.tile([P, 2, H], BF16, name="mc")
+        words = {}
+        for name, src, col0, bblk, blocks in gates:
+            for g in range(G):
+                flat = src[g].rearrange("p n t -> p (n t)")
+                pieces = blocks if (name == "o" and g == G - 1) else [(0, H)]
+                for c0, n in pieces:
+                    w = keep.tile([P, n], U32, name="w_%s_%d_%d" % (name, g, c0), align_bytes=64)
+                    nc.sync.dma_start(
+                        out=w[:].bitcast(I32),
+                        in_=flat[:, 4 * (col0 + c0) : 4 * (col0 + c0 + n)].bitcast(I32),
+                    )
+                    words[(name, g, c0)] = w
+            if name == "f":
+                nc.sync.dma_start(out=mc[:], in_=mailbox_c)
+
+        bias_bc = keep.tile([P, 12, 512], BF16, name="bias_bc")
+
+        def spread_bias(j, eng):
+            pb = psum.tile([P, 512], F32, name="pb_%d" % j, tag="bank")
+            nc.tensor.matmul(pb[:], lhsT=ident[:, j : j + 1].to_broadcast([P, P]), rhs=brow[:], start=True, stop=True)
+            if eng == 0:
+                nc.scalar.copy(out=bias_bc[:, j, :], in_=pb[:])
+            else:
+                nc.vector.tensor_copy(out=bias_bc[:, j, :], in_=pb[:])
+
+        for j in (9, 10, 11):
+            spread_bias(j, 0)
+
+        hc = keep.tile([P, 2 * H], BF16, name="hc", tag="hc")
+        nc.vector.tensor_tensor(out=hc[:, 0:H], in0=mh[:, 0, :], in1=mh[:, 1, :], op=ALU.add)
+        nc.vector.tensor_tensor(out=hc[:, H : 2 * H], in0=mh[:, 0, :], in1=mh[:, 1, :], op=ALU.max)
+
+        grouped = keep.tile([P, G, P, 4], BF16, name="grouped", align_bytes=64)
+        for g in range(G):
+            xt = psum.tile([P, 4, P], BF16, name="xt_%d" % g, tag="bank")
+            for t in range(4):
+                nc.tensor.transpose(xt[:, t, :], hc[:, 512 * g + t : 512 * (g + 1) : 4], ident[:])
+            if g % 2 == 0:
+                nc.vector.tensor_copy(out=grouped[:, g, :, :], in_=xt[:].rearrange("p t m -> p m t"))
+            else:
+                nc.scalar.copy(out=grouped[:, g, :, :], in_=xt[:].rearrange("p t m -> p m t"))
+
+        hcodes = keep.tile([P, G * P], U32, name="hcodes", align_bytes=64)
+        hscale = keep.tile([P, G * P], U8, name="hscale", align_bytes=64)
+        gflat = grouped[:].rearrange("p g m t -> p (g m t)")
+        for a in range(3):
+            nc.vector.quantize_mx(
+                out=hcodes[:, 256 * a : 256 * (a + 1)].bitcast(FP8X4),
+                scales=hscale[:, 256 * a : 256 * (a + 1)],
+                in_=gflat[:, 1024 * a : 1024 * (a + 1)],
+            )
+
+        for n, j in enumerate((0, 1, 2, 6, 7, 8, 3, 4, 5)):
+            spread_bias(j, n % 2)
+
+        mcsum = keep.tile([P, H], F32, name="mcsum")
+        nc.vector.tensor_tensor(out=mcsum[:], in0=mc[:, 0, :], in1=mc[:, 1, :], op=ALU.add)
+
+        i_s = keep.tile([P, H], F32, name="i_s", tag="hc")
+        tch = keep.tile([P, H], F32, name="tch", tag="mh")
+        outsb = keep.tile([P, 2 * H], F32, name="outsb")
+        bflat = bias_bc[:].rearrange("p j n -> p (j n)")
+
+        for name, src, col0, bblk, blocks in gates:
+            plane = pf if name == "f" else piou
+            accs = {}
+            for c0, n in blocks:
+                accs[c0] = psum.tile([P, n], F32, name="acc_%s_%d" % (name, c0), tag="bank")
+            for g in range(G):
+                a, slot = (0, g) if g < 4 else (1, g - 4)
+                for c0, n in blocks:
+                    if (name, g, c0) in words and words[(name, g, c0)].shape[1] == n:
+                        rhs = words[(name, g, c0)][:]
+                    else:
+                        rhs = words[(name, g, 0)][:, c0 : c0 + n]
+                    nc.tensor.matmul_mx(
+                        out=accs[c0][:],
+                        lhsT=hcodes[:, P * g : P * (g + 1)].bitcast(FP8X4),
+                        lhsT_scale=hscale[:, P * g : P * (g + 1)],
+                        rhs=rhs.bitcast(FP8X4),
+                        rhs_scale=plane[4 * slot : P, a, col0 + c0 : col0 + c0 + n],
+                        start=(g == 0),
+                        stop=(g == G - 1),
+                    )
+            for c0, n in blocks:
+                cols = slice(c0, c0 + n)
+                pre = work.tile([P, 512], F32, name="pre", tag="pre")
+                nc.vector.tensor_tensor(
+                    out=pre[:, 0:n], in0=accs[c0][:], in1=bflat[:, 512 * bblk + c0 : 512 * bblk + c0 + n], op=ALU.add
+                )
+                if name == "f":
+                    act = work.tile([P, 512], F32, name="act", tag="act")
+                    nc.scalar.activation(out=act[:, 0:n], in_=pre[:, 0:n], func=ACT.Sigmoid)
+                    nc.vector.tensor_tensor(out=mcsum[:, cols], in0=act[:, 0:n], in1=mcsum[:, cols], op=ALU.mult)
+                elif name == "i":
+                    nc.scalar.activation(out=i_s[:, cols], in_=pre[:, 0:n], func=ACT.Sigmoid)
+                elif name == "u":
+                    act = work.tile([P, 512], F32, name="act", tag="act")
+                    nc.scalar.activation(out=act[:, 0:n], in_=pre[:, 0:n], func=ACT.Tanh)
+                    nc.vector.tensor_tensor(out=i_s[:, cols], in0=act[:, 0:n], in1=i_s[:, cols], op=ALU.mult)
+                    nc.vector.tensor_tensor(
+                        out=outsb[:, H + c0 : H + c0 + n], in0=i_s[:, cols], in1=mcsum[:, cols], op=ALU.add
+                    )
+                    nc.scalar.activation(out=tch[:, cols], in_=outsb[:, H + c0 : H + c0 + n], func=ACT.Tanh)
+                else:
+                    act = work.tile([P, 512], F32, name="act", tag="act")
+                    nc.scalar.activation(out=act[:, 0:n], in_=pre[:, 0:n], func=ACT.Sigmoid)
+                    nc.vector.tensor_tensor(out=outsb[:, cols], in0=act[:, 0:n], in1=tch[:, cols], op=ALU.mult)
+                    nc.sync.dma_start(out=out[:, cols], in_=outsb[:, cols])
+            if name == "u":
+                nc.sync.dma_start(out=out[:, H : 2 * H], in_=outsb[:, H : 2 * H])

@@ -17,7 +17,7 @@ H = 1536
 G = 6
 FLOPS = 2 * 128 * (2 * H) * (4 * H)
 
-SCALES_ON_GPSIMD = True
+SCALES_ON_GPSIMD = False
 
 
 def tile_treelstmcellv2_w_kernel(

@@ -17,8 +17,6 @@ H = 1536
 G = 6
 FLOPS = 2 * 128 * (2 * H) * (4 * H)
 
-SCALES_ON_GPSIMD = False
-
 
 def tile_treelstmcellv2_w_kernel(
     tc, mailbox_h, mailbox_c, U_iou_w_words, U_iou_w_scales, b_iou, U_f_w_words, U_f_w_scales, U_f_b, out
@@ -41,30 +39,27 @@ def tile_treelstmcellv2_w_kernel(
         pf = keep.tile([P, 2, H], U8, name="pf", align_bytes=64)
         piou = keep.tile([P, 2, 3 * H], U8, name="piou", align_bytes=64)
         brow = keep.tile([P, 512], BF16, name="brow")
-        nc.vector.memset(brow[:].bitcast(I32), 0)
         nc.vector.memset(pf[:].bitcast(I32), 0)
-        nc.vector.memset(piou[:].bitcast(I32), 0)
+        nc.vector.memset(piou[:, 0, :].bitcast(I32), 0)
+        nc.vector.memset(piou[:, 1, :].bitcast(I32), 0)
+        nc.vector.memset(brow[:].bitcast(I32), 0)
         ident = keep.tile([P, P], BF16, name="ident")
         make_identity(nc, ident[:])
 
         mh = keep.tile([P, 2, H], BF16, name="mh", tag="mh")
-        nc.sync.dma_start(out=mh[:], in_=mailbox_h)
         nc.scalar.dma_start(out=brow[0:9, :], in_=b_iou.rearrange("o (j n) -> (o j) n", n=512))
         nc.scalar.dma_start(out=brow[9:12, :], in_=U_f_b.rearrange("(j n) -> j n", n=512))
 
-        def load_planes(plane, scales):
-            for a, g0, g1 in ((0, 0, 4), (1, 4, 6)):
-                rows = 4 * (g1 - g0)
-                for q in range(4):
-                    dst = plane[32 * q : 32 * q + rows, a, :]
-                    src = scales[g0:g1, 4 * q : 4 * q + 4, :]
-                    if SCALES_ON_GPSIMD:
-                        nc.gpsimd.dma_start(out=dst.bitcast(F32), in_=src.bitcast(F32))
-                    else:
-                        nc.sync.dma_start(out=dst.bitcast(I32), in_=src.bitcast(I32))
-
-        load_planes(pf, U_f_w_scales)
-        load_planes(piou, U_iou_w_scales)
+        for quads in ((2, 3), (0, 1)):
+            for plane, scales in ((pf, U_f_w_scales), (piou, U_iou_w_scales)):
+                for a, g0, g1 in ((0, 0, 4), (1, 4, 6)):
+                    rows = 4 * (g1 - g0)
+                    for q in quads:
+                        nc.sync.dma_start(
+                            out=plane[32 * q : 32 * q + rows, a, :].bitcast(I32),
+                            in_=scales[g0:g1, 4 * q : 4 * q + 4, :].bitcast(I32),
+                        )
+        nc.sync.dma_start(out=mh[:], in_=mailbox_h)
 
         mc = keep.tile([P, 2, H], BF16, name="mc")
         words = {}

@@ -50,6 +50,8 @@ def tile_treelstmcellv2_w_kernel(
         nc.scalar.dma_start(out=brow[0:9, :], in_=b_iou.rearrange("o (j n) -> (o j) n", n=512))
         nc.scalar.dma_start(out=brow[9:12, :], in_=U_f_b.rearrange("(j n) -> j n", n=512))
 
+        nc.sync.dma_start(out=mh[:], in_=mailbox_h)
+
         for quads in ((2, 3), (0, 1)):
             for plane, scales in ((pf, U_f_w_scales), (piou, U_iou_w_scales)):
                 for a, g0, g1 in ((0, 0, 4), (1, 4, 6)):
@@ -59,7 +61,6 @@ def tile_treelstmcellv2_w_kernel(
                             out=plane[32 * q : 32 * q + rows, a, :].bitcast(I32),
                             in_=scales[g0:g1, 4 * q : 4 * q + 4, :].bitcast(I32),
                         )
-        nc.sync.dma_start(out=mh[:], in_=mailbox_h)
 
         mc = keep.tile([P, 2, H], BF16, name="mc")
         words = {}

@@ -26,6 +26,7 @@ def tile_treelstmcellv2_w_kernel(
         keep = ctx.enter_context(tc.tile_pool(name="keep", bufs=1))
         work = ctx.enter_context(tc.tile_pool(name="work", bufs=3))
         psum = ctx.enter_context(tc.psum_pool(name="psum", bufs=8))
+        ctx.enter_context(tc.manual_schedule(engines={mybir.EngineType.SP}))
 
         full = [(0, 512), (512, 512), (1024, 512)]
         tail = [(0, 512), (512, 512), (1024, 256), (1280, 256)]
@@ -54,13 +55,17 @@ def tile_treelstmcellv2_w_kernel(
 
         for quads in ((2, 3), (0, 1)):
             for plane, scales in ((pf, U_f_w_scales), (piou, U_iou_w_scales)):
-                for a, g0, g1 in ((0, 0, 4), (1, 4, 6)):
-                    rows = 4 * (g1 - g0)
-                    for q in quads:
-                        nc.sync.dma_start(
-                            out=plane[32 * q : 32 * q + rows, a, :].bitcast(I32),
-                            in_=scales[g0:g1, 4 * q : 4 * q + 4, :].bitcast(I32),
-                        )
+                for q in quads:
+                    nc.sync.dma_start(
+                        out=plane[32 * q : 32 * q + 16, 0, :].bitcast(I32),
+                        in_=scales[0:4, 4 * q : 4 * q + 4, :].bitcast(I32),
+                    )
+        for plane, scales in ((pf, U_f_w_scales), (piou, U_iou_w_scales)):
+            for q in (2, 3, 0, 1):
+                nc.gpsimd.dma_start(
+                    out=plane[32 * q : 32 * q + 8, 1, :].bitcast(F32),
+                    in_=scales[4:6, 4 * q : 4 * q + 4, :].bitcast(F32),
+                )
 
         mc = keep.tile([P, 2, H], BF16, name="mc")
         words = {}

@@ -70,16 +70,27 @@ def tile_treelstmcellv2_w_kernel(
         mc = keep.tile([P, 2, H], BF16, name="mc")
         words = {}
         for name, src, col0, bblk, blocks in gates:
-            for g in range(G):
-                flat = src[g].rearrange("p n t -> p (n t)")
-                pieces = blocks if (name == "o" and g == G - 1) else [(0, H)]
-                for c0, n in pieces:
-                    w = keep.tile([P, n], U32, name="w_%s_%d_%d" % (name, g, c0), align_bytes=64)
-                    nc.sync.dma_start(
-                        out=w[:].bitcast(I32),
-                        in_=flat[:, 4 * (col0 + c0) : 4 * (col0 + c0 + n)].bitcast(I32),
-                    )
-                    words[(name, g, c0)] = w
+            for g in range(0, G, 2):
+                split_last = name == "o" and g == G - 2
+                if split_last:
+                    flat = src[g].rearrange("p n t -> p (n t)")
+                    w = keep.tile([P, H], U32, name="w_%s_%d" % (name, g), align_bytes=64)
+                    nc.sync.dma_start(out=w[:].bitcast(I32), in_=flat[:, 4 * col0 : 4 * (col0 + H)].bitcast(I32))
+                    words[(name, g)] = w[:]
+                    flat = src[g + 1].rearrange("p n t -> p (n t)")
+                    for c0, n in blocks:
+                        w = keep.tile([P, n], U32, name="w_%s_%d_%d" % (name, g + 1, c0), align_bytes=64)
+                        nc.sync.dma_start(
+                            out=w[:].bitcast(I32),
+                            in_=flat[:, 4 * (col0 + c0) : 4 * (col0 + c0 + n)].bitcast(I32),
+                        )
+                        words[(name, g + 1, c0)] = w[:]
+                else:
+                    pair = src[g : g + 2].rearrange("g p n t -> p g (n t)")
+                    w = keep.tile([P, 2, H], U32, name="w_%s_%d" % (name, g), align_bytes=64)
+                    nc.sync.dma_start(out=w[:].bitcast(I32), in_=pair[:, :, 4 * col0 : 4 * (col0 + H)].bitcast(I32))
+                    words[(name, g)] = w[:, 0, :]
+                    words[(name, g + 1)] = w[:, 1, :]
             if name == "f":
                 nc.sync.dma_start(out=mc[:], in_=mailbox_c)
 
@@ -139,10 +150,10 @@ def tile_treelstmcellv2_w_kernel(
             for g in range(G):
                 a, slot = (0, g) if g < 4 else (1, g - 4)
                 for c0, n in blocks:
-                    if (name, g, c0) in words and words[(name, g, c0)].shape[1] == n:
-                        rhs = words[(name, g, c0)][:]
+                    if (name, g, c0) in words:
+                        rhs = words[(name, g, c0)]
                     else:
-                        rhs = words[(name, g, 0)][:, c0 : c0 + n]
+                        rhs = words[(name, g)][:, c0 : c0 + n]
                     nc.tensor.matmul_mx(
                         out=accs[c0][:],
                         lhsT=hcodes[:, P * g : P * (g + 1)].bitcast(FP8X4),

@@ -73,18 +73,15 @@ def tile_treelstmcellv2_w_kernel(
             for g in range(0, G, 2):
                 split_last = name == "o" and g == G - 2
                 if split_last:
-                    flat = src[g].rearrange("p n t -> p (n t)")
-                    w = keep.tile([P, H], U32, name="w_%s_%d" % (name, g), align_bytes=64)
-                    nc.sync.dma_start(out=w[:].bitcast(I32), in_=flat[:, 4 * col0 : 4 * (col0 + H)].bitcast(I32))
-                    words[(name, g)] = w[:]
-                    flat = src[g + 1].rearrange("p n t -> p (n t)")
+                    pair = src[g : g + 2].rearrange("g p n t -> p g (n t)")
                     for c0, n in blocks:
-                        w = keep.tile([P, n], U32, name="w_%s_%d_%d" % (name, g + 1, c0), align_bytes=64)
+                        w = keep.tile([P, 2, n], U32, name="w_%s_%d_%d" % (name, g, c0), align_bytes=64)
                         nc.sync.dma_start(
                             out=w[:].bitcast(I32),
-                            in_=flat[:, 4 * (col0 + c0) : 4 * (col0 + c0 + n)].bitcast(I32),
+                            in_=pair[:, :, 4 * (col0 + c0) : 4 * (col0 + c0 + n)].bitcast(I32),
                         )
-                        words[(name, g + 1, c0)] = w[:]
+                        words[(name, g, c0)] = w[:, 0, :]
+                        words[(name, g + 1, c0)] = w[:, 1, :]
                 else:
                     pair = src[g : g + 2].rearrange("g p n t -> p g (n t)")
                     w = keep.tile([P, 2, H], U32, name="w_%s_%d" % (name, g), align_bytes=64)
@@ -147,22 +144,25 @@ def tile_treelstmcellv2_w_kernel(
             accs = {}
             for c0, n in blocks:
                 accs[c0] = psum.tile([P, n], F32, name="acc_%s_%d" % (name, c0), tag="bank")
-            for g in range(G):
+            order = [(g, c0, n) for g in range(G) for c0, n in blocks]
+            if name == "o":
+                order = [(g, c0, n) for g in range(G - 2) for c0, n in blocks]
+                order += [(g, c0, n) for c0, n in blocks for g in (G - 2, G - 1)]
+            for g, c0, n in order:
                 a, slot = (0, g) if g < 4 else (1, g - 4)
-                for c0, n in blocks:
-                    if (name, g, c0) in words:
-                        rhs = words[(name, g, c0)]
-                    else:
-                        rhs = words[(name, g)][:, c0 : c0 + n]
-                    nc.tensor.matmul_mx(
-                        out=accs[c0][:],
-                        lhsT=hcodes[:, P * g : P * (g + 1)].bitcast(FP8X4),
-                        lhsT_scale=hscale[:, P * g : P * (g + 1)],
-                        rhs=rhs.bitcast(FP8X4),
-                        rhs_scale=plane[4 * slot : P, a, col0 + c0 : col0 + c0 + n],
-                        start=(g == 0),
-                        stop=(g == G - 1),
-                    )
+                if (name, g, c0) in words:
+                    rhs = words[(name, g, c0)]
+                else:
+                    rhs = words[(name, g)][:, c0 : c0 + n]
+                nc.tensor.matmul_mx(
+                    out=accs[c0][:],
+                    lhsT=hcodes[:, P * g : P * (g + 1)].bitcast(FP8X4),
+                    lhsT_scale=hscale[:, P * g : P * (g + 1)],
+                    rhs=rhs.bitcast(FP8X4),
+                    rhs_scale=plane[4 * slot : P, a, col0 + c0 : col0 + c0 + n],
+                    start=(g == 0),
+                    stop=(g == G - 1),
+                )
             for c0, n in blocks:
                 cols = slice(c0, c0 + n)
                 pre = work.tile([P, 512], F32, name="pre", tag="pre")

from contextlib import ExitStack

import concourse.mybir as mybir
from concourse.masks import make_identity

BF16 = mybir.dt.bfloat16
F32 = mybir.dt.float32
I32 = mybir.dt.int32
U32 = mybir.dt.uint32
U8 = mybir.dt.uint8
FP8X4 = mybir.dt.float8_e4m3fn_x4
ALU = mybir.AluOpType
ACT = mybir.ActivationFunctionType

P = 128
H = 1536
G = 6
FLOPS = 2 * 128 * (2 * H) * (4 * H)


def tile_treelstmcellv2_w_kernel(
    tc, mailbox_h, mailbox_c, U_iou_w_words, U_iou_w_scales, b_iou, U_f_w_words, U_f_w_scales, U_f_b, out
):
    nc = tc.nc
    with ExitStack() as ctx:
        keep = ctx.enter_context(tc.tile_pool(name="keep", bufs=1))
        work = ctx.enter_context(tc.tile_pool(name="work", bufs=3))
        psum = ctx.enter_context(tc.psum_pool(name="psum", bufs=8))
        ctx.enter_context(tc.manual_schedule(engines={mybir.EngineType.SP}))

        full = [(0, 512), (512, 512), (1024, 512)]
        tail = [(0, 512), (512, 512), (1024, 256), (1280, 256)]
        gates = [
            ("f", U_f_w_words, 0, 9, full),
            ("i", U_iou_w_words, 0, 0, full),
            ("u", U_iou_w_words, 2 * H, 6, full),
            ("o", U_iou_w_words, H, 3, tail),
        ]

        pf = keep.tile([P, 2, H], U8, name="pf", align_bytes=64)
        piou = keep.tile([P, 2, 3 * H], U8, name="piou", align_bytes=64)
        brow = keep.tile([P, 512], BF16, name="brow")
        nc.vector.memset(pf[:].bitcast(I32), 0)
        nc.vector.memset(piou[:, 0, :].bitcast(I32), 0)
        nc.vector.memset(piou[:, 1, :].bitcast(I32), 0)
        nc.vector.memset(brow[:].bitcast(I32), 0)
        ident = keep.tile([P, P], BF16, name="ident")
        make_identity(nc, ident[:])

        mh = keep.tile([P, 2, H], BF16, name="mh", tag="mh")
        nc.scalar.dma_start(out=brow[0:9, :], in_=b_iou.rearrange("o (j n) -> (o j) n", n=512))
        nc.scalar.dma_start(out=brow[9:12, :], in_=U_f_b.rearrange("(j n) -> j n", n=512))

        nc.sync.dma_start(out=mh[:], in_=mailbox_h)

        for quads in ((2, 3), (0, 1)):
            for plane, scales in ((pf, U_f_w_scales), (piou, U_iou_w_scales)):
                for q in quads:
                    nc.sync.dma_start(
                        out=plane[32 * q : 32 * q + 16, 0, :].bitcast(I32),
                        in_=scales[0:4, 4 * q : 4 * q + 4, :].bitcast(I32),
                    )
        for plane, scales in ((pf, U_f_w_scales), (piou, U_iou_w_scales)):
            for q in (2, 3, 0, 1):
                nc.gpsimd.dma_start(
                    out=plane[32 * q : 32 * q + 8, 1, :].bitcast(F32),
                    in_=scales[4:6, 4 * q : 4 * q + 4, :].bitcast(F32),
                )

        mc = keep.tile([P, 2, H], BF16, name="mc")
        words = {}
        for name, src, col0, bblk, blocks in gates:
            for g in range(0, G, 2):
                split_last = name == "o" and g == G - 2
                if split_last:
                    pair = src[g : g + 2].rearrange("g p n t -> p g (n t)")
                    for c0, n in blocks:
                        w = keep.tile([P, 2, n], U32, name="w_%s_%d_%d" % (name, g, c0), align_bytes=64)
                        nc.sync.dma_start(
                            out=w[:].bitcast(I32),
                            in_=pair[:, :, 4 * (col0 + c0) : 4 * (col0 + c0 + n)].bitcast(I32),
                        )
                        words[(name, g, c0)] = w[:, 0, :]
                        words[(name, g + 1, c0)] = w[:, 1, :]
                else:
                    pair = src[g : g + 2].rearrange("g p n t -> p g (n t)")
                    w = keep.tile([P, 2, H], U32, name="w_%s_%d" % (name, g), align_bytes=64)
                    nc.sync.dma_start(out=w[:].bitcast(I32), in_=pair[:, :, 4 * col0 : 4 * (col0 + H)].bitcast(I32))
                    words[(name, g)] = w[:, 0, :]
                    words[(name, g + 1)] = w[:, 1, :]
            if name == "f":
                nc.sync.dma_start(out=mc[:], in_=mailbox_c)

        bias_bc = keep.tile([P, 12, 512], BF16, name="bias_bc")

        def spread_bias(j, eng):
            pb = psum.tile([P, 512], F32, name="pb_%d" % j, tag="bank")
            nc.tensor.matmul(pb[:], lhsT=ident[:, j : j + 1].to_broadcast([P, P]), rhs=brow[:], start=True, stop=True)
            if eng == 0:
                nc.scalar.copy(out=bias_bc[:, j, :], in_=pb[:])
            else:
                nc.vector.tensor_copy(out=bias_bc[:, j, :], in_=pb[:])

        for j in (9, 10, 11):
            spread_bias(j, 0)

        hc = keep.tile([P, 2 * H], BF16, name="hc", tag="hc")
        nc.vector.tensor_tensor(out=hc[:, 0:H], in0=mh[:, 0, :], in1=mh[:, 1, :], op=ALU.add)
        nc.vector.tensor_tensor(out=hc[:, H : 2 * H], in0=mh[:, 0, :], in1=mh[:, 1, :], op=ALU.max)

        grouped = keep.tile([P, G, P, 4], BF16, name="grouped", align_bytes=64)
        for g in range(G):
            xt = psum.tile([P, 4, P], BF16, name="xt_%d" % g, tag="bank")
            for t in range(4):
                nc.tensor.transpose(xt[:, t, :], hc[:, 512 * g + t : 512 * (g + 1) : 4], ident[:])
            if g % 2 == 0:
                nc.vector.tensor_copy(out=grouped[:, g, :, :], in_=xt[:].rearrange("p t m -> p m t"))
            else:
                nc.scalar.copy(out=grouped[:, g, :, :], in_=xt[:].rearrange("p t m -> p m t"))

        hcodes = keep.tile([P, G * P], U32, name="hcodes", align_bytes=64)
        hscale = keep.tile([P, G * P], U8, name="hscale", align_bytes=64)
        gflat = grouped[:].rearrange("p g m t -> p (g m t)")
        for a in range(3):
            nc.vector.quantize_mx(
                out=hcodes[:, 256 * a : 256 * (a + 1)].bitcast(FP8X4),
                scales=hscale[:, 256 * a : 256 * (a + 1)],
                in_=gflat[:, 1024 * a : 1024 * (a + 1)],
            )

        for n, j in enumerate((0, 1, 2, 6, 7, 8, 3, 4, 5)):
            spread_bias(j, n % 2)

        mcsum = keep.tile([P, H], F32, name="mcsum")
        nc.vector.tensor_tensor(out=mcsum[:], in0=mc[:, 0, :], in1=mc[:, 1, :], op=ALU.add)

        i_s = keep.tile([P, H], F32, name="i_s", tag="hc")
        tch = keep.tile([P, H], F32, name="tch", tag="mh")
        outsb = keep.tile([P, 2 * H], F32, name="outsb")
        bflat = bias_bc[:].rearrange("p j n -> p (j n)")

        for name, src, col0, bblk, blocks in gates:
            plane = pf if name == "f" else piou
            accs = {}
            for c0, n in blocks:
                accs[c0] = psum.tile([P, n], F32, name="acc_%s_%d" % (name, c0), tag="bank")
            order = [(g, c0, n) for g in range(G) for c0, n in blocks]
            if name == "o":
                order = [(g, c0, n) for g in range(G - 2) for c0, n in blocks]
                order += [(g, c0, n) for c0, n in blocks for g in (G - 2, G - 1)]
            for g, c0, n in order:
                a, slot = (0, g) if g < 4 else (1, g - 4)
                if (name, g, c0) in words:
                    rhs = words[(name, g, c0)]
                else:
                    rhs = words[(name, g)][:, c0 : c0 + n]
                nc.tensor.matmul_mx(
                    out=accs[c0][:],
                    lhsT=hcodes[:, P * g : P * (g + 1)].bitcast(FP8X4),
                    lhsT_scale=hscale[:, P * g : P * (g + 1)],
                    rhs=rhs.bitcast(FP8X4),
                    rhs_scale=plane[4 * slot : P, a, col0 + c0 : col0 + c0 + n],
                    start=(g == 0),
                    stop=(g == G - 1),
                )
            for c0, n in blocks:
                cols = slice(c0, c0 + n)
                pre = work.tile([P, 512], F32, name="pre", tag="pre")
                nc.vector.tensor_tensor(
                    out=pre[:, 0:n], in0=accs[c0][:], in1=bflat[:, 512 * bblk + c0 : 512 * bblk + c0 + n], op=ALU.add
                )
                if name == "f":
                    act = work.tile([P, 512], F32, name="act", tag="act")
                    nc.scalar.activation(out=act[:, 0:n], in_=pre[:, 0:n], func=ACT.Sigmoid)
                    nc.vector.tensor_tensor(out=mcsum[:, cols], in0=act[:, 0:n], in1=mcsum[:, cols], op=ALU.mult)
                elif name == "i":
                    nc.scalar.activation(out=i_s[:, cols], in_=pre[:, 0:n], func=ACT.Sigmoid)
                elif name == "u":
                    act = work.tile([P, 512], F32, name="act", tag="act")
                    nc.scalar.activation(out=act[:, 0:n], in_=pre[:, 0:n], func=ACT.Tanh)
                    nc.vector.tensor_tensor(out=i_s[:, cols], in0=act[:, 0:n], in1=i_s[:, cols], op=ALU.mult)
                    nc.vector.tensor_tensor(
                        out=outsb[:, H + c0 : H + c0 + n], in0=i_s[:, cols], in1=mcsum[:, cols], op=ALU.add
                    )
                    nc.scalar.activation(out=tch[:, cols], in_=outsb[:, H + c0 : H + c0 + n], func=ACT.Tanh)
                else:
                    act = work.tile([P, 512], F32, name="act", tag="act")
                    nc.scalar.activation(out=act[:, 0:n], in_=pre[:, 0:n], func=ACT.Sigmoid)
                    nc.vector.tensor_tensor(out=outsb[:, cols], in0=act[:, 0:n], in1=tch[:, cols], op=ALU.mult)
                    nc.sync.dma_start(out=out[:, cols], in_=outsb[:, cols])
            if name == "u":
                nc.sync.dma_start(out=out[:, H : 2 * H], in_=outsb[:, H : 2 * H])
